import numpy as np
import ml_dtypes


def mxq(x, axis, fmt="e4m3"):
    dtype, down = {"e4m3": (ml_dtypes.float8_e4m3fn, 7), "e5m2": (ml_dtypes.float8_e5m2, 14)}[fmt]
    v = np.moveaxis(np.asarray(x, np.float32).astype(ml_dtypes.bfloat16).astype(np.float64), axis, -1)
    blocks = v.reshape(v.shape[:-1] + (-1, 32))
    amax = np.abs(blocks).max(-1, keepdims=True)
    byte = np.maximum(np.where(amax > 0, np.frexp(amax)[1] - 1 + 127, 0) - down, 1)
    scale = np.exp2(byte - 127.0)
    codes = (blocks / scale).astype(np.float32).astype(dtype).astype(np.float64)
    return np.moveaxis((codes * scale).reshape(v.shape), -1, axis)


WIDE = False


def mx_kscale(k):
    if not WIDE:
        return np.ones(k)
    levels = np.array([10, -10, 5, -5, 0])
    if k % 512:
        return np.exp2(np.random.permutation(np.resize(levels, k // 32))).repeat(32)
    a = np.empty((k // 512, 16))
    for p in range(k // 512):
        a[p, :8] = np.random.permutation(np.resize(levels, 8))
        for g in range(8):
            far = levels[np.abs(levels - a[p, g]) >= 10]
            a[p, g + 8] = far[np.random.randint(len(far))]
    return np.exp2(a.ravel()).repeat(32)


BF16 = ml_dtypes.bfloat16


def bf(x):
    return np.asarray(x, np.float32).astype(BF16)


def f64(x):
    return np.asarray(x).astype(np.float64)


M, B, I, H, O = 5, 2048, 128, 512, 64
O2 = 2 * O
EPS = 1e-6


def softplus(v):
    return np.maximum(v, 0.0) + np.log(1.0 + np.exp(-np.abs(v)))


def setup_inputs():
    s, t = mx_kscale(H), mx_kscale(H)
    return {"h1": bf(np.maximum(np.random.standard_normal((M, B, H)), 0.0) * s),
            "W2": bf(np.random.standard_normal((M, H, H)) * 1.4 / np.sqrt(H) * t[None, :, None] / s[None, None, :]),
            "b2": bf(np.random.standard_normal((M, H)) * 0.3 * t),
            "W3": bf(np.random.standard_normal((M, O2, H)) * 1.4 / np.sqrt(H) / t[None, None, :]),
            "b3": bf(np.random.standard_normal((M, O2)) * 0.3)}


def reference(h1, W2, b2, W3, b3):
    h2 = np.maximum((mxq(f64(h1), 2, "e4m3") @ mxq(f64(W2), 2, "e4m3").transpose(0, 2, 1)) + f64(b2)[:, None, :], 0.0)
    y = (mxq(h2, 2, "e4m3") @ mxq(f64(W3), 2, "e4m3").transpose(0, 2, 1)) + f64(b3)[:, None, :]
    means = y[:, :, :O]
    variances = softplus(y[:, :, O:]) + EPS
    mean = means.mean(axis=0)
    variance = (variances + means ** 2).mean(axis=0) - mean ** 2
    variance = np.maximum(variance, 0.0) + EPS
    return mean, variance

@@ -1,0 +1,382 @@
+from contextlib import ExitStack
+
+import concourse.mybir as mybir
+from concourse.masks import make_identity
+
+NM, B, H, O = 5, 2048, 512, 64
+O2 = 2 * O
+FLOPS = 2 * NM * B * H * (H + O2)
+
+F32 = mybir.dt.float32
+BF16 = mybir.dt.bfloat16
+U32 = mybir.dt.uint32
+U8 = mybir.dt.uint8
+FP8X4 = mybir.dt.float8_e4m3fn_x4
+ACT = mybir.ActivationFunctionType
+ALU = mybir.AluOpType
+
+P = 128
+CH = 512
+NCH = B // CH
+NS = NCH * NM
+RAW_BUFS = 8
+BANK_DT = F32
+
+
+def tile_gaussianmixturemlp_pa_kernel(tc, h1, W2, b2, W3, b3, out_0, out_1):
+    nc = tc.nc
+    with ExitStack() as ctx:
+        const = ctx.enter_context(tc.tile_pool(name="const", bufs=1))
+        rawp = ctx.enter_context(tc.tile_pool(name="rawp", bufs=RAW_BUFS))
+        work = ctx.enter_context(tc.tile_pool(name="work", bufs=2))
+        tp = ctx.enter_context(tc.psum_pool(name="tp", bufs=2))
+        s1 = ctx.enter_context(tc.psum_pool(name="s1", bufs=4))
+        s2 = ctx.enter_context(tc.psum_pool(name="s2", bufs=1))
+        aux = ctx.enter_context(tc.psum_pool(name="aux", bufs=1))
+        ctx.enter_context(tc.manual_schedule())
+
+        ident = const.tile([P, P], F32, name="ident", tag="ident")
+        warm = const.tile([P, 1], F32, name="warm", tag="warm")
+        warm2 = const.tile([P, 1], F32, name="warm2", tag="warm2")
+        b2c = const.tile([P, NM, 4], BF16, name="b2c", tag="b2c")
+        b3b = const.tile([P, NM, O2], BF16, name="b3b", tag="b3b")
+        w3raw = const.tile([P, NM, H], BF16, name="w3raw", tag="w3raw")
+        w3g = const.tile([P, NM * O2, 4], BF16, name="w3g", tag="w3g", align_bytes=64)
+        w2c = const.tile([P, NM, H], U32, name="w2c", tag="w2c", align_bytes=64)
+        w2s = const.tile([P, NM, H], U8, name="w2s", tag="w2s", align_bytes=64)
+        w3c = const.tile([P, NM * O2], U32, name="w3c", tag="w3c", align_bytes=64)
+        w3s = const.tile([P, NM * O2], U8, name="w3s", tag="w3s", align_bytes=64)
+        accp = const.tile([P, NCH, 4, O], F32, name="accp", tag="accp")
+        upre = const.tile([P, NCH, 4, O], F32, name="upre", tag="upre")
+        lnp = const.tile([P, NCH, 4, O], F32, name="lnp", tag="lnp")
+        wv = const.tile([P, NCH, 4, O], F32, name="wv", tag="wv")
+        var_sb = const.tile([P, NCH, 4, O], F32, name="var_sb", tag="var_sb")
+        bsum = const.tile([P, O], F32, name="bsum", tag="bsum")
+        bbar = const.tile([P, 1, O], F32, name="bbar", tag="bbar")
+
+        nc.vector.memset(warm[:], 0.0)
+        nc.scalar.activation(out=warm2[:], in_=warm[:], func=ACT.Exp)
+        make_identity(nc, ident[:])
+        nc.scalar.dma_start(out=b2c[:], in_=b2.rearrange("m (p t) -> p m t", t=4))
+
+        raw_w2 = {}
+        raw_h1 = {}
+        loads = []
+        for i in range(NM):
+            loads.append(("w2", i))
+            loads.append(("h1", i))
+            if i == 1:
+                loads.append(("w3", 0))
+        for i in range(NM, NS):
+            loads.append(("h1", i))
+        state = {"next": 0, "slots": RAW_BUFS}
+
+        def pump():
+            while state["next"] < len(loads):
+                kind, i = loads[state["next"]]
+                if kind == "w3":
+                    nc.sync.dma_start(out=w3raw[:], in_=W3.rearrange("m o k -> o m k"))
+                else:
+                    if state["slots"] == 0:
+                        return
+                    state["slots"] = state["slots"] - 1
+                    t = rawp.tile([P, 4, H], BF16, name="raw_%s%d" % (kind, i), tag="raw")
+                    if kind == "w2":
+                        nc.sync.dma_start(out=t[:], in_=W2[i].rearrange("(p t) k -> p t k", t=4))
+                        raw_w2[i] = t
+                    else:
+                        c, m = i // NM, i % NM
+                        nc.sync.dma_start(
+                            out=t[:],
+                            in_=h1[m, c * CH:(c + 1) * CH, :].rearrange("(p j) k -> p j k", j=4),
+                        )
+                        raw_h1[i] = t
+                state["next"] = state["next"] + 1
+
+        def freed():
+            state["slots"] = state["slots"] + 1
+            pump()
+
+        def transposes(pool, tag, words, w_first, count):
+            xt = pool.tile([P, 2, 256], F32, name="xt_%s" % tag, tag=tag)
+            for jj in range(count):
+                w0 = w_first + 256 * jj
+                for u in range(2):
+                    nc.tensor.transpose(
+                        xt[:, u, P * jj:P * (jj + 1)], words[:, w0 + u:w0 + 256:2], ident[:]
+                    )
+            return xt
+
+        def copy_out(on_scalar, grouped, n0, xt, ncols):
+            gw = grouped[:].rearrange("p n t -> p (n t)").bitcast(F32)
+            dst = gw[:, 2 * n0:2 * (n0 + ncols)].rearrange("p (r u) -> p r u", u=2)
+            src = xt[:, :, 0:ncols].rearrange("p u r -> p r u")
+            if on_scalar:
+                nc.scalar.copy(out=dst, in_=src)
+            else:
+                nc.vector.tensor_copy(out=dst, in_=src)
+
+        def words_of(t):
+            return t[:].rearrange("p j k -> p (j k)").bitcast(F32)
+
+        xt_h1 = {}
+        g1 = {}
+        c1 = {}
+        sc1 = {}
+        bank = {}
+        h2raw = {}
+        g2 = {}
+        c2 = {}
+        sc2 = {}
+        pbank = {}
+        ys = {}
+        sqs = {}
+        exs = {}
+        accs = {}
+        psums = {}
+        wgs = {}
+        xt_w = {}
+
+        def st_a(s):
+            w = words_of(raw_h1[s])
+            xt_h1[s] = []
+            for half in range(2):
+                xt_h1[s].append(transposes(tp, "xt", w, 512 * half, 2))
+            freed()
+
+        def on_vector(s):
+            return s % NM in (1, 3)
+
+        def st_b(s):
+            g1[s] = work.tile([P, CH, 4], BF16, name="g1", tag="g1", bufs=2, align_bytes=64)
+            copy_out(True, g1[s], 0, xt_h1[s][0], 256)
+            if not on_vector(s):
+                copy_out(True, g1[s], 256, xt_h1[s][1], 256)
+
+        def st_bv(s):
+            if on_vector(s):
+                copy_out(False, g1[s], 256, xt_h1[s][1], 256)
+
+        def st_c(s):
+            c1[s] = work.tile([P, CH], U32, name="c1", tag="c1", bufs=3, align_bytes=64)
+            sc1[s] = work.tile([P, CH], U8, name="sc1", tag="sc1", bufs=3, align_bytes=64)
+            nc.vector.quantize_mx(
+                out=c1[s][:].bitcast(FP8X4), scales=sc1[s][:],
+                in_=g1[s][:].rearrange("p n t -> p (n t)"),
+            )
+
+        def st_d(s):
+            m = s % NM
+            bank[s] = []
+            for t in range(4):
+                ps = s1.tile([P, CH], BANK_DT, name="bank", tag="bank")
+                nc.tensor.matmul_mx(
+                    out=ps[:],
+                    lhsT=w2c[:, m, P * t:P * (t + 1)].bitcast(FP8X4),
+                    lhsT_scale=w2s[:, m, P * t:P * (t + 1)],
+                    rhs=c1[s][:].bitcast(FP8X4),
+                    rhs_scale=sc1[s][:],
+                    start=True, stop=True,
+                )
+                bank[s].append(ps)
+
+        def st_e(s):
+            m = s % NM
+            h2raw[s] = work.tile([P, 4, CH], BF16, name="h2raw", tag="h2raw", bufs=3)
+            for t in range(4):
+                nc.scalar.activation(
+                    out=h2raw[s][:, t, :], in_=bank[s][t][:], func=ACT.Relu,
+                    bias=b2c[:, m, t:t + 1], scale=1.0,
+                )
+
+        def st_f(s):
+            g2[s] = work.tile([P, CH, 4], BF16, name="g2", tag="g2", bufs=2, align_bytes=64)
+            nc.vector.tensor_copy(out=g2[s][:], in_=h2raw[s][:].rearrange("p t n -> p n t"))
+
+        def st_g(s):
+            c2[s] = work.tile([P, CH], U32, name="c2", tag="c2", bufs=7, align_bytes=64)
+            sc2[s] = work.tile([P, CH], U8, name="sc2", tag="sc2", bufs=7, align_bytes=64)
+            nc.vector.quantize_mx(
+                out=c2[s][:].bitcast(FP8X4), scales=sc2[s][:],
+                in_=g2[s][:].rearrange("p n t -> p (n t)"),
+            )
+
+        def st_h(s):
+            m = s % NM
+            pbank[s] = s2.tile([P, 4, O2], F32, name="pbank", tag="pbank")
+            for j in range(4):
+                nc.tensor.matmul_mx(
+                    out=pbank[s][:, j, :],
+                    lhsT=c2[s][:, P * j:P * (j + 1)].bitcast(FP8X4),
+                    lhsT_scale=sc2[s][:, P * j:P * (j + 1)],
+                    rhs=w3c[:, O2 * m:O2 * (m + 1)].bitcast(FP8X4),
+                    rhs_scale=w3s[:, O2 * m:O2 * (m + 1)],
+                    start=True, stop=True,
+                )
+
+        def st_hsum(c):
+            psums[c] = aux.tile([P, 4, O2], F32, name="psum_all", tag="xw")
+            for j in range(4):
+                for m in range(NM):
+                    s = c * NM + m
+                    nc.tensor.matmul_mx(
+                        out=psums[c][:, j, :],
+                        lhsT=c2[s][:, P * j:P * (j + 1)].bitcast(FP8X4),
+                        lhsT_scale=sc2[s][:, P * j:P * (j + 1)],
+                        rhs=w3c[:, O2 * m:O2 * (m + 1)].bitcast(FP8X4),
+                        rhs_scale=w3s[:, O2 * m:O2 * (m + 1)],
+                        start=(m == 0), stop=(m == NM - 1),
+                    )
+
+        def bias_mean():
+            nc.vector.tensor_reduce(
+                out=bsum[:], in_=b3b[:, :, 0:O].rearrange("p m o -> p o m"),
+                axis=mybir.AxisListType.X, op=ALU.add)
+            nc.vector.tensor_scalar(
+                out=bbar[:, 0, :], in0=bsum[:], scalar1=0.2, scalar2=None, op0=ALU.mult)
+
+        def st_i(s):
+            m = s % NM
+            ys[s] = work.tile([P, 4, O2], F32, name="ys", tag="ys", bufs=4)
+            nc.vector.tensor_tensor(
+                out=ys[s][:], in0=pbank[s][:],
+                in1=b3b[:, m:m + 1, :].to_broadcast([P, 4, O2]), op=ALU.add,
+            )
+
+        def st_js(s):
+            sqs[s] = work.tile([P, 4, O], F32, name="sqs", tag="sqs", bufs=2)
+            ab = work.tile([P, 4, O], F32, name="ab", tag="ab", bufs=2)
+            exs[s] = work.tile([P, 4, O], F32, name="exs", tag="exs", bufs=2)
+            nc.scalar.activation(out=sqs[s][:], in_=ys[s][:, :, 0:O], func=ACT.Square)
+            nc.scalar.activation(out=ab[:], in_=ys[s][:, :, O:O2], func=ACT.Abs)
+            nc.scalar.activation(out=exs[s][:], in_=ab[:], func=ACT.Exp, scale=-1.0)
+
+        def st_jv(s):
+            c, m = s // NM, s % NM
+            v = ys[s][:, :, O:O2]
+            if m == 0:
+                accs[c] = work.tile([P, 4, O], F32, name="accs", tag="accs", bufs=2)
+                nc.vector.scalar_tensor_tensor(
+                    out=accs[c][:], in0=v, scalar=0.0, in1=sqs[s][:], op0=ALU.max, op1=ALU.add)
+                nc.vector.tensor_scalar(
+                    out=accp[:, c], in0=exs[s][:], scalar1=1.0, scalar2=None, op0=ALU.add)
+                return
+            nc.vector.scalar_tensor_tensor(
+                out=accs[c][:], in0=v, scalar=0.0, in1=accs[c][:], op0=ALU.max, op1=ALU.add)
+            nc.vector.scalar_tensor_tensor(
+                out=accp[:, c], in0=exs[s][:], scalar=1.0, in1=accp[:, c], op0=ALU.add, op1=ALU.mult)
+            nc.vector.tensor_tensor(out=accs[c][:], in0=sqs[s][:], in1=accs[c][:], op=ALU.add)
+            if m == NM - 1:
+                mean_sb = work.tile([P, 4, O], F32, name="mean_sb", tag="mean_sb", bufs=2)
+                msq = work.tile([P, 4, O], F32, name="msq", tag="msq", bufs=2)
+                nc.vector.scalar_tensor_tensor(
+                    out=mean_sb[:], in0=psums[c][:, :, 0:O], scalar=0.2,
+                    in1=bbar[:].to_broadcast([P, 4, O]), op0=ALU.mult, op1=ALU.add)
+                nc.vector.tensor_tensor(out=msq[:], in0=mean_sb[:], in1=mean_sb[:], op=ALU.mult)
+                nc.vector.scalar_tensor_tensor(
+                    out=upre[:, c], in0=accs[c][:], scalar=0.2, in1=msq[:],
+                    op0=ALU.mult, op1=ALU.subtract)
+                nc.sync.dma_start(
+                    out=out_0[c * CH:(c + 1) * CH, :].rearrange("(p j) o -> p j o", j=4),
+                    in_=mean_sb[:])
+
+        def flat(t, c0, c1_):
+            return t[:, c0:c1_].rearrange("p c j o -> p (c j o)")
+
+        def fin_ln(c0, c1_):
+            nc.scalar.activation(out=flat(lnp, c0, c1_), in_=flat(accp, c0, c1_), func=ACT.Ln)
+
+        def fin_v(c0, c1_):
+            nc.vector.scalar_tensor_tensor(
+                out=flat(wv, c0, c1_), in0=flat(lnp, c0, c1_), scalar=0.2, in1=flat(upre, c0, c1_),
+                op0=ALU.mult, op1=ALU.add)
+            nc.vector.tensor_scalar(
+                out=flat(var_sb, c0, c1_), in0=flat(wv, c0, c1_), scalar1=-1e-6, scalar2=2e-6,
+                op0=ALU.max, op1=ALU.add)
+            nc.sync.dma_start(
+                out=out_1.rearrange("(c p j) o -> p c (j o)", c=NCH, j=4)[:, c0:c1_, :],
+                in_=var_sb[:, c0:c1_].rearrange("p c j o -> p c (j o)"))
+
+        def w2_t(m, half):
+            xt_w[(m, half)] = transposes(aux, "xw", words_of(raw_w2[m]), 512 * half, 2)
+            if half == 1:
+                freed()
+
+        def w2_copy(m, half):
+            if half == 0:
+                wgs[m] = work.tile([P, H, 4], BF16, name="wg", tag="wg", bufs=2, align_bytes=64)
+            copy_out(half == 0, wgs[m], 256 * half, xt_w[(m, half)], 256)
+
+        def w2_q(m):
+            nc.vector.quantize_mx(
+                out=w2c[:, m, :].bitcast(FP8X4), scales=w2s[:, m, :],
+                in_=wgs[m][:].rearrange("p n t -> p (n t)"),
+            )
+
+        def w3_prep(q):
+            count = min(2, NM - 2 * q)
+            ncols = P * count
+            w = w3raw[:].rearrange("p m k -> p (m k)").bitcast(F32)
+            xt = transposes(aux, "xw", w, 512 * q, count)
+            copy_out(False, w3g, 256 * q, xt, ncols)
+            nc.vector.quantize_mx(
+                out=w3c[:, 256 * q:256 * q + ncols].bitcast(FP8X4),
+                scales=w3s[:, 256 * q:256 * q + ncols],
+                in_=w3g[:].rearrange("p n t -> p (n t)")[:, 1024 * q:1024 * q + 4 * ncols],
+            )
+
+        def ok(s):
+            return 0 <= s < NS
+
+        pump()
+        for k in range(-2, NS + 3):
+            wm = k + 2
+            has_w = 0 <= wm < NM
+            if ok(k + 1):
+                st_b(k + 1)
+            if k == 0:
+                nc.scalar.dma_start(
+                    out=b3b[:].rearrange("p m o -> p (m o)"),
+                    in_=b3.rearrange("m o -> (m o)").partition_broadcast(P),
+                )
+            if has_w:
+                w2_t(wm, 0)
+                w2_copy(wm, 0)
+            if ok(k):
+                st_d(k)
+            if ok(k - 2) and k < NS:
+                st_i(k - 2)
+            if k == 3:
+                bias_mean()
+            if ok(k + 1):
+                st_bv(k + 1)
+            if ok(k - 1):
+                st_f(k - 1)
+            if ok(k - 2) and k >= NS:
+                st_i(k - 2)
+            if ok(k + 1):
+                st_c(k + 1)
+            if ok(k + 2):
+                st_a(k + 2)
+            if ok(k - 1):
+                st_g(k - 1)
+            if has_w:
+                w2_t(wm, 1)
+                w2_copy(wm, 1)
+                w2_q(wm)
+            if 0 <= k + 1 < 3:
+                w3_prep(k + 1)
+            if ok(k - 1):
+                st_h(k - 1)
+                if (k - 1) % NM == NM - 1:
+                    st_hsum((k - 1) // NM)
+            if ok(k - 3):
+                st_js(k - 3)
+            if ok(k):
+                st_e(k)
+            if ok(k - 3):
+                st_jv(k - 3)
+        fin_ln(0, NCH - 1)
+        fin_ln(NCH - 1, NCH)
+        fin_v(0, NCH - 1)
+        fin_v(NCH - 1, NCH)

@@ -54,6 +54,10 @@ def tile_gaussianmixturemlp_pa_kernel(tc, h1, W2, b2, W3, b3, out_0, out_1):
         bsum = const.tile([P, O], F32, name="bsum", tag="bsum")
         bbar = const.tile([P, 1, O], F32, name="bbar", tag="bbar")
 
+        zl = const.tile([P, P], BF16, name="zl", tag="zl")
+        zr = const.tile([P, CH], BF16, name="zr", tag="zr")
+        nc.vector.memset(zl[:], 0.0)
+        nc.vector.memset(zr[:], 0.0)
         nc.vector.memset(warm[:], 0.0)
         nc.scalar.activation(out=warm2[:], in_=warm[:], func=ACT.Exp)
         make_identity(nc, ident[:])
@@ -61,13 +65,11 @@ def tile_gaussianmixturemlp_pa_kernel(tc, h1, W2, b2, W3, b3, out_0, out_1):
 
         raw_w2 = {}
         raw_h1 = {}
-        loads = []
-        for i in range(NM):
+        loads = [("w2", 0), ("h1", 0), ("h1", 1), ("w2", 1), ("h1", 2), ("w3", 0)]
+        for i in range(2, NM):
             loads.append(("w2", i))
-            loads.append(("h1", i))
-            if i == 1:
-                loads.append(("w3", 0))
-        for i in range(NM, NS):
+            loads.append(("h1", i + 1))
+        for i in range(NM + 1, NS):
             loads.append(("h1", i))
         state = {"next": 0, "slots": RAW_BUFS}
 
@@ -134,28 +136,22 @@ def tile_gaussianmixturemlp_pa_kernel(tc, h1, W2, b2, W3, b3, out_0, out_1):
         exs = {}
         accs = {}
         psums = {}
+        means = {}
+        msqs = {}
         wgs = {}
         xt_w = {}
 
-        def st_a(s):
-            w = words_of(raw_h1[s])
-            xt_h1[s] = []
-            for half in range(2):
-                xt_h1[s].append(transposes(tp, "xt", w, 512 * half, 2))
-            freed()
-
-        def on_vector(s):
-            return s % NM in (1, 3)
+        def st_a(s, half):
+            if half == 0:
+                xt_h1[s] = []
+            xt_h1[s].append(transposes(tp, "xt", words_of(raw_h1[s]), 512 * half, 2))
+            if half == 1:
+                freed()
 
         def st_b(s):
             g1[s] = work.tile([P, CH, 4], BF16, name="g1", tag="g1", bufs=2, align_bytes=64)
-            copy_out(True, g1[s], 0, xt_h1[s][0], 256)
-            if not on_vector(s):
-                copy_out(True, g1[s], 256, xt_h1[s][1], 256)
-
-        def st_bv(s):
-            if on_vector(s):
-                copy_out(False, g1[s], 256, xt_h1[s][1], 256)
+            for half in range(2):
+                copy_out(True, g1[s], 256 * half, xt_h1[s][half], 256)
 
         def st_c(s):
             c1[s] = work.tile([P, CH], U32, name="c1", tag="c1", bufs=3, align_bytes=64)
@@ -165,10 +161,11 @@ def tile_gaussianmixturemlp_pa_kernel(tc, h1, W2, b2, W3, b3, out_0, out_1):
                 in_=g1[s][:].rearrange("p n t -> p (n t)"),
             )
 
-        def st_d(s):
+        def st_d(s, ts):
             m = s % NM
-            bank[s] = []
-            for t in range(4):
+            if ts[0] == 0:
+                bank[s] = []
+            for t in ts:
                 ps = s1.tile([P, CH], BANK_DT, name="bank", tag="bank")
                 nc.tensor.matmul_mx(
                     out=ps[:],
@@ -201,9 +198,29 @@ def tile_gaussianmixturemlp_pa_kernel(tc, h1, W2, b2, W3, b3, out_0, out_1):
                 in_=g2[s][:].rearrange("p n t -> p (n t)"),
             )
 
+        def plain_dummy(n):
+            for i in range(n):
+                junk = s1.tile([P, CH], F32, name="junk", tag="bank")
+                nc.tensor.matmul(out=junk[:], lhsT=zl[:], rhs=zr[:], start=True, stop=True)
+
+        def get_pbank(s):
+            if s not in pbank:
+                pbank[s] = s2.tile([P, 4, O2], F32, name="pbank", tag="pbank")
+            return pbank[s]
+
+        def mx_dummy(s):
+            nc.tensor.matmul_mx(
+                out=get_pbank(s)[:].rearrange("p j o -> p (j o)"),
+                lhsT=c2[s - 1][:, 0:P].bitcast(FP8X4),
+                lhsT_scale=sc2[s - 1][:, 0:P],
+                rhs=w3c[:, 0:CH].bitcast(FP8X4),
+                rhs_scale=w3s[:, 0:CH],
+                start=True, stop=True,
+            )
+
         def st_h(s):
             m = s % NM
-            pbank[s] = s2.tile([P, 4, O2], F32, name="pbank", tag="pbank")
+            get_pbank(s)
             for j in range(4):
                 nc.tensor.matmul_mx(
                     out=pbank[s][:, j, :],
@@ -247,38 +264,41 @@ def tile_gaussianmixturemlp_pa_kernel(tc, h1, W2, b2, W3, b3, out_0, out_1):
             sqs[s] = work.tile([P, 4, O], F32, name="sqs", tag="sqs", bufs=2)
             ab = work.tile([P, 4, O], F32, name="ab", tag="ab", bufs=2)
             exs[s] = work.tile([P, 4, O], F32, name="exs", tag="exs", bufs=2)
-            nc.scalar.activation(out=sqs[s][:], in_=ys[s][:, :, 0:O], func=ACT.Square)
             nc.scalar.activation(out=ab[:], in_=ys[s][:, :, O:O2], func=ACT.Abs)
             nc.scalar.activation(out=exs[s][:], in_=ab[:], func=ACT.Exp, scale=-1.0)
+            nc.scalar.activation(out=sqs[s][:], in_=ys[s][:, :, 0:O], func=ACT.Square)
+
+        def st_mean(c):
+            means[c] = work.tile([P, 4, O], F32, name="mean_sb", tag="mean_sb", bufs=2)
+            msqs[c] = work.tile([P, 4, O], F32, name="msq", tag="msq", bufs=2)
+            nc.vector.scalar_tensor_tensor(
+                out=means[c][:], in0=psums[c][:, :, 0:O], scalar=0.2,
+                in1=bbar[:].to_broadcast([P, 4, O]), op0=ALU.mult, op1=ALU.add)
+            nc.sync.dma_start(
+                out=out_0[c * CH:(c + 1) * CH, :].rearrange("(p j) o -> p j o", j=4),
+                in_=means[c][:])
 
         def st_jv(s):
             c, m = s // NM, s % NM
             v = ys[s][:, :, O:O2]
             if m == 0:
                 accs[c] = work.tile([P, 4, O], F32, name="accs", tag="accs", bufs=2)
-                nc.vector.scalar_tensor_tensor(
-                    out=accs[c][:], in0=v, scalar=0.0, in1=sqs[s][:], op0=ALU.max, op1=ALU.add)
                 nc.vector.tensor_scalar(
                     out=accp[:, c], in0=exs[s][:], scalar1=1.0, scalar2=None, op0=ALU.add)
+                nc.vector.scalar_tensor_tensor(
+                    out=accs[c][:], in0=v, scalar=0.0, in1=sqs[s][:], op0=ALU.max, op1=ALU.add)
                 return
             nc.vector.scalar_tensor_tensor(
-                out=accs[c][:], in0=v, scalar=0.0, in1=accs[c][:], op0=ALU.max, op1=ALU.add)
-            nc.vector.scalar_tensor_tensor(
                 out=accp[:, c], in0=exs[s][:], scalar=1.0, in1=accp[:, c], op0=ALU.add, op1=ALU.mult)
+            nc.vector.scalar_tensor_tensor(
+                out=accs[c][:], in0=v, scalar=0.0, in1=accs[c][:], op0=ALU.max, op1=ALU.add)
+            if m == NM - 1:
+                nc.vector.tensor_tensor(out=msqs[c][:], in0=means[c][:], in1=means[c][:], op=ALU.mult)
             nc.vector.tensor_tensor(out=accs[c][:], in0=sqs[s][:], in1=accs[c][:], op=ALU.add)
             if m == NM - 1:
-                mean_sb = work.tile([P, 4, O], F32, name="mean_sb", tag="mean_sb", bufs=2)
-                msq = work.tile([P, 4, O], F32, name="msq", tag="msq", bufs=2)
                 nc.vector.scalar_tensor_tensor(
-                    out=mean_sb[:], in0=psums[c][:, :, 0:O], scalar=0.2,
-                    in1=bbar[:].to_broadcast([P, 4, O]), op0=ALU.mult, op1=ALU.add)
-                nc.vector.tensor_tensor(out=msq[:], in0=mean_sb[:], in1=mean_sb[:], op=ALU.mult)
-                nc.vector.scalar_tensor_tensor(
-                    out=upre[:, c], in0=accs[c][:], scalar=0.2, in1=msq[:],
+                    out=upre[:, c], in0=accs[c][:], scalar=0.2, in1=msqs[c][:],
                     op0=ALU.mult, op1=ALU.subtract)
-                nc.sync.dma_start(
-                    out=out_0[c * CH:(c + 1) * CH, :].rearrange("(p j) o -> p j o", j=4),
-                    in_=mean_sb[:])
 
         def flat(t, c0, c1_):
             return t[:, c0:c1_].rearrange("p c j o -> p (c j o)")
@@ -286,10 +306,12 @@ def tile_gaussianmixturemlp_pa_kernel(tc, h1, W2, b2, W3, b3, out_0, out_1):
         def fin_ln(c0, c1_):
             nc.scalar.activation(out=flat(lnp, c0, c1_), in_=flat(accp, c0, c1_), func=ACT.Ln)
 
-        def fin_v(c0, c1_):
+        def fin_w(c0, c1_):
             nc.vector.scalar_tensor_tensor(
                 out=flat(wv, c0, c1_), in0=flat(lnp, c0, c1_), scalar=0.2, in1=flat(upre, c0, c1_),
                 op0=ALU.mult, op1=ALU.add)
+
+        def fin_v(c0, c1_):
             nc.vector.tensor_scalar(
                 out=flat(var_sb, c0, c1_), in0=flat(wv, c0, c1_), scalar1=-1e-6, scalar2=2e-6,
                 op0=ALU.max, op1=ALU.add)
@@ -329,9 +351,21 @@ def tile_gaussianmixturemlp_pa_kernel(tc, h1, W2, b2, W3, b3, out_0, out_1):
             return 0 <= s < NS
 
         pump()
-        for k in range(-2, NS + 3):
-            wm = k + 2
-            has_w = 0 <= wm < NM
+        plain_dummy(6)
+        w2_t(0, 0)
+        w2_copy(0, 0)
+        plain_dummy(2)
+        w2_t(0, 1)
+        w2_copy(0, 1)
+        w2_q(0)
+        plain_dummy(2)
+        st_a(0, 0)
+        st_a(0, 1)
+        plain_dummy(2)
+        for k in range(-1, NS + 3):
+            wm = k + 1
+            has_w = 1 <= wm < NM
+            junk_ok = 2 <= k <= NS
             if ok(k + 1):
                 st_b(k + 1)
             if k == 0:
@@ -339,37 +373,49 @@ def tile_gaussianmixturemlp_pa_kernel(tc, h1, W2, b2, W3, b3, out_0, out_1):
                     out=b3b[:].rearrange("p m o -> p (m o)"),
                     in_=b3.rearrange("m o -> (m o)").partition_broadcast(P),
                 )
-            if has_w:
-                w2_t(wm, 0)
-                w2_copy(wm, 0)
-            if ok(k):
-                st_d(k)
             if ok(k - 2) and k < NS:
                 st_i(k - 2)
             if k == 3:
                 bias_mean()
-            if ok(k + 1):
-                st_bv(k + 1)
             if ok(k - 1):
                 st_f(k - 1)
             if ok(k - 2) and k >= NS:
                 st_i(k - 2)
+            if ok(k - 2) and (k - 2) % NM == NM - 1:
+                st_mean((k - 2) // NM)
             if ok(k + 1):
                 st_c(k + 1)
-            if ok(k + 2):
-                st_a(k + 2)
             if ok(k - 1):
                 st_g(k - 1)
+            if ok(k):
+                st_d(k, [0, 1])
+            if has_w:
+                w2_t(wm, 0)
+                w2_copy(wm, 0)
+            if ok(k + 2):
+                st_a(k + 2, 0)
+            if ok(k):
+                st_d(k, [2])
+            if junk_ok:
+                mx_dummy(k - 1)
             if has_w:
                 w2_t(wm, 1)
                 w2_copy(wm, 1)
                 w2_q(wm)
-            if 0 <= k + 1 < 3:
-                w3_prep(k + 1)
+            if ok(k + 2):
+                st_a(k + 2, 1)
+            if ok(k):
+                st_d(k, [3])
+            if 0 <= k < 3:
+                w3_prep(k)
+            if junk_ok:
+                mx_dummy(k - 1)
             if ok(k - 1):
                 st_h(k - 1)
                 if (k - 1) % NM == NM - 1:
                     st_hsum((k - 1) // NM)
+            if k < 0:
+                plain_dummy(2)
             if ok(k - 3):
                 st_js(k - 3)
             if ok(k):
@@ -378,5 +424,7 @@ def tile_gaussianmixturemlp_pa_kernel(tc, h1, W2, b2, W3, b3, out_0, out_1):
                 st_jv(k - 3)
         fin_ln(0, NCH - 1)
         fin_ln(NCH - 1, NCH)
+        fin_w(0, NCH - 1)
+        fin_w(NCH - 1, NCH)
         fin_v(0, NCH - 1)
         fin_v(NCH - 1, NCH)

@@ -265,8 +265,8 @@ def tile_gaussianmixturemlp_pa_kernel(tc, h1, W2, b2, W3, b3, out_0, out_1):
             ab = work.tile([P, 4, O], F32, name="ab", tag="ab", bufs=2)
             exs[s] = work.tile([P, 4, O], F32, name="exs", tag="exs", bufs=2)
             nc.scalar.activation(out=ab[:], in_=ys[s][:, :, O:O2], func=ACT.Abs)
-            nc.scalar.activation(out=exs[s][:], in_=ab[:], func=ACT.Exp, scale=-1.0)
             nc.scalar.activation(out=sqs[s][:], in_=ys[s][:, :, 0:O], func=ACT.Square)
+            nc.scalar.activation(out=exs[s][:], in_=ab[:], func=ACT.Exp, scale=-1.0)
 
         def st_mean(c):
             means[c] = work.tile([P, 4, O], F32, name="mean_sb", tag="mean_sb", bufs=2)
@@ -277,6 +277,14 @@ def tile_gaussianmixturemlp_pa_kernel(tc, h1, W2, b2, W3, b3, out_0, out_1):
             nc.sync.dma_start(
                 out=out_0[c * CH:(c + 1) * CH, :].rearrange("(p j) o -> p j o", j=4),
                 in_=means[c][:])
+
+        def st_msq(c):
+            nc.vector.tensor_tensor(out=msqs[c][:], in0=means[c][:], in1=means[c][:], op=ALU.mult)
+
+        def st_u(c):
+            nc.vector.scalar_tensor_tensor(
+                out=upre[:, c], in0=accs[c][:], scalar=0.2, in1=msqs[c][:],
+                op0=ALU.mult, op1=ALU.subtract)
 
         def st_jv(s):
             c, m = s // NM, s % NM
@@ -289,16 +297,10 @@ def tile_gaussianmixturemlp_pa_kernel(tc, h1, W2, b2, W3, b3, out_0, out_1):
                     out=accs[c][:], in0=v, scalar=0.0, in1=sqs[s][:], op0=ALU.max, op1=ALU.add)
                 return
             nc.vector.scalar_tensor_tensor(
-                out=accp[:, c], in0=exs[s][:], scalar=1.0, in1=accp[:, c], op0=ALU.add, op1=ALU.mult)
-            nc.vector.scalar_tensor_tensor(
                 out=accs[c][:], in0=v, scalar=0.0, in1=accs[c][:], op0=ALU.max, op1=ALU.add)
-            if m == NM - 1:
-                nc.vector.tensor_tensor(out=msqs[c][:], in0=means[c][:], in1=means[c][:], op=ALU.mult)
+            nc.vector.scalar_tensor_tensor(
+                out=accp[:, c], in0=exs[s][:], scalar=1.0, in1=accp[:, c], op0=ALU.add, op1=ALU.mult)
             nc.vector.tensor_tensor(out=accs[c][:], in0=sqs[s][:], in1=accs[c][:], op=ALU.add)
-            if m == NM - 1:
-                nc.vector.scalar_tensor_tensor(
-                    out=upre[:, c], in0=accs[c][:], scalar=0.2, in1=msqs[c][:],
-                    op0=ALU.mult, op1=ALU.subtract)
 
         def flat(t, c0, c1_):
             return t[:, c0:c1_].rearrange("p c j o -> p (c j o)")
@@ -366,6 +368,7 @@ def tile_gaussianmixturemlp_pa_kernel(tc, h1, W2, b2, W3, b3, out_0, out_1):
             wm = k + 1
             has_w = 1 <= wm < NM
             junk_ok = 2 <= k <= NS
+            chunk_mean = ok(k - 2) and (k - 2) % NM == NM - 1
             if ok(k + 1):
                 st_b(k + 1)
             if k == 0:
@@ -375,18 +378,22 @@ def tile_gaussianmixturemlp_pa_kernel(tc, h1, W2, b2, W3, b3, out_0, out_1):
                 )
             if ok(k - 2) and k < NS:
                 st_i(k - 2)
+            if ok(k - 4) and (k - 4) % NM == NM - 1:
+                st_u((k - 4) // NM)
             if k == 3:
                 bias_mean()
+            if chunk_mean and k < NS:
+                st_mean((k - 2) // NM)
             if ok(k - 1):
                 st_f(k - 1)
             if ok(k - 2) and k >= NS:
                 st_i(k - 2)
-            if ok(k - 2) and (k - 2) % NM == NM - 1:
+            if chunk_mean and k >= NS:
                 st_mean((k - 2) // NM)
             if ok(k + 1):
                 st_c(k + 1)
-            if ok(k - 1):
-                st_g(k - 1)
+            if chunk_mean and k < NS:
+                st_msq((k - 2) // NM)
             if ok(k):
                 st_d(k, [0, 1])
             if has_w:
@@ -401,6 +408,9 @@ def tile_gaussianmixturemlp_pa_kernel(tc, h1, W2, b2, W3, b3, out_0, out_1):
             if has_w:
                 w2_t(wm, 1)
                 w2_copy(wm, 1)
+            if ok(k - 1):
+                st_g(k - 1)
+            if has_w:
                 w2_q(wm)
             if ok(k + 2):
                 st_a(k + 2, 1)
@@ -422,6 +432,9 @@ def tile_gaussianmixturemlp_pa_kernel(tc, h1, W2, b2, W3, b3, out_0, out_1):
                 st_e(k)
             if ok(k - 3):
                 st_jv(k - 3)
+            if chunk_mean and k >= NS:
+                st_msq((k - 2) // NM)
+        st_u(NCH - 1)
         fin_ln(0, NCH - 1)
         fin_ln(NCH - 1, NCH)
         fin_w(0, NCH - 1)

from contextlib import ExitStack

import concourse.mybir as mybir
from concourse.masks import make_identity

NM, B, H, O = 5, 2048, 512, 64
O2 = 2 * O
FLOPS = 2 * NM * B * H * (H + O2)

F32 = mybir.dt.float32
BF16 = mybir.dt.bfloat16
U32 = mybir.dt.uint32
U8 = mybir.dt.uint8
FP8X4 = mybir.dt.float8_e4m3fn_x4
ACT = mybir.ActivationFunctionType
ALU = mybir.AluOpType

P = 128
CH = 512
NCH = B // CH
NS = NCH * NM
RAW_BUFS = 8
BANK_DT = F32


def tile_gaussianmixturemlp_pa_kernel(tc, h1, W2, b2, W3, b3, out_0, out_1):
    nc = tc.nc
    with ExitStack() as ctx:
        const = ctx.enter_context(tc.tile_pool(name="const", bufs=1))
        rawp = ctx.enter_context(tc.tile_pool(name="rawp", bufs=RAW_BUFS))
        work = ctx.enter_context(tc.tile_pool(name="work", bufs=2))
        tp = ctx.enter_context(tc.psum_pool(name="tp", bufs=2))
        s1 = ctx.enter_context(tc.psum_pool(name="s1", bufs=4))
        s2 = ctx.enter_context(tc.psum_pool(name="s2", bufs=1))
        aux = ctx.enter_context(tc.psum_pool(name="aux", bufs=1))
        ctx.enter_context(tc.manual_schedule())

        ident = const.tile([P, P], F32, name="ident", tag="ident")
        warm = const.tile([P, 1], F32, name="warm", tag="warm")
        warm2 = const.tile([P, 1], F32, name="warm2", tag="warm2")
        b2c = const.tile([P, NM, 4], BF16, name="b2c", tag="b2c")
        b3b = const.tile([P, NM, O2], BF16, name="b3b", tag="b3b")
        w3raw = const.tile([P, NM, H], BF16, name="w3raw", tag="w3raw")
        w3g = const.tile([P, NM * O2, 4], BF16, name="w3g", tag="w3g", align_bytes=64)
        w2c = const.tile([P, NM, H], U32, name="w2c", tag="w2c", align_bytes=64)
        w2s = const.tile([P, NM, H], U8, name="w2s", tag="w2s", align_bytes=64)
        w3c = const.tile([P, NM * O2], U32, name="w3c", tag="w3c", align_bytes=64)
        w3s = const.tile([P, NM * O2], U8, name="w3s", tag="w3s", align_bytes=64)
        accp = const.tile([P, NCH, 4, O], F32, name="accp", tag="accp")
        upre = const.tile([P, NCH, 4, O], F32, name="upre", tag="upre")
        lnp = const.tile([P, NCH, 4, O], F32, name="lnp", tag="lnp")
        wv = const.tile([P, NCH, 4, O], F32, name="wv", tag="wv")
        var_sb = const.tile([P, NCH, 4, O], F32, name="var_sb", tag="var_sb")
        bsum = const.tile([P, O], F32, name="bsum", tag="bsum")
        bbar = const.tile([P, 1, O], F32, name="bbar", tag="bbar")

        zl = const.tile([P, P], BF16, name="zl", tag="zl")
        zr = const.tile([P, CH], BF16, name="zr", tag="zr")
        nc.vector.memset(zl[:], 0.0)
        nc.vector.memset(zr[:], 0.0)
        nc.vector.memset(warm[:], 0.0)
        nc.scalar.activation(out=warm2[:], in_=warm[:], func=ACT.Exp)
        make_identity(nc, ident[:])
        nc.scalar.dma_start(out=b2c[:], in_=b2.rearrange("m (p t) -> p m t", t=4))

        raw_w2 = {}
        raw_h1 = {}
        loads = [("w2", 0), ("h1", 0), ("h1", 1), ("w2", 1), ("h1", 2), ("w3", 0)]
        for i in range(2, NM):
            loads.append(("w2", i))
            loads.append(("h1", i + 1))
        for i in range(NM + 1, NS):
            loads.append(("h1", i))
        state = {"next": 0, "slots": RAW_BUFS}

        def pump():
            while state["next"] < len(loads):
                kind, i = loads[state["next"]]
                if kind == "w3":
                    nc.sync.dma_start(out=w3raw[:], in_=W3.rearrange("m o k -> o m k"))
                else:
                    if state["slots"] == 0:
                        return
                    state["slots"] = state["slots"] - 1
                    t = rawp.tile([P, 4, H], BF16, name="raw_%s%d" % (kind, i), tag="raw")
                    if kind == "w2":
                        nc.sync.dma_start(out=t[:], in_=W2[i].rearrange("(p t) k -> p t k", t=4))
                        raw_w2[i] = t
                    else:
                        c, m = i // NM, i % NM
                        nc.sync.dma_start(
                            out=t[:],
                            in_=h1[m, c * CH:(c + 1) * CH, :].rearrange("(p j) k -> p j k", j=4),
                        )
                        raw_h1[i] = t
                state["next"] = state["next"] + 1

        def freed():
            state["slots"] = state["slots"] + 1
            pump()

        def transposes(pool, tag, words, w_first, count):
            xt = pool.tile([P, 2, 256], F32, name="xt_%s" % tag, tag=tag)
            for jj in range(count):
                w0 = w_first + 256 * jj
                for u in range(2):
                    nc.tensor.transpose(
                        xt[:, u, P * jj:P * (jj + 1)], words[:, w0 + u:w0 + 256:2], ident[:]
                    )
            return xt

        def copy_out(on_scalar, grouped, n0, xt, ncols):
            gw = grouped[:].rearrange("p n t -> p (n t)").bitcast(F32)
            dst = gw[:, 2 * n0:2 * (n0 + ncols)].rearrange("p (r u) -> p r u", u=2)
            src = xt[:, :, 0:ncols].rearrange("p u r -> p r u")
            if on_scalar:
                nc.scalar.copy(out=dst, in_=src)
            else:
                nc.vector.tensor_copy(out=dst, in_=src)

        def words_of(t):
            return t[:].rearrange("p j k -> p (j k)").bitcast(F32)

        xt_h1 = {}
        g1 = {}
        c1 = {}
        sc1 = {}
        bank = {}
        h2raw = {}
        g2 = {}
        c2 = {}
        sc2 = {}
        pbank = {}
        ys = {}
        sqs = {}
        exs = {}
        accs = {}
        psums = {}
        means = {}
        msqs = {}
        wgs = {}
        xt_w = {}

        def st_a(s, half):
            if half == 0:
                xt_h1[s] = []
            xt_h1[s].append(transposes(tp, "xt", words_of(raw_h1[s]), 512 * half, 2))
            if half == 1:
                freed()

        def st_b(s):
            g1[s] = work.tile([P, CH, 4], BF16, name="g1", tag="g1", bufs=2, align_bytes=64)
            for half in range(2):
                copy_out(True, g1[s], 256 * half, xt_h1[s][half], 256)

        def st_c(s):
            c1[s] = work.tile([P, CH], U32, name="c1", tag="c1", bufs=3, align_bytes=64)
            sc1[s] = work.tile([P, CH], U8, name="sc1", tag="sc1", bufs=3, align_bytes=64)
            nc.vector.quantize_mx(
                out=c1[s][:].bitcast(FP8X4), scales=sc1[s][:],
                in_=g1[s][:].rearrange("p n t -> p (n t)"),
            )

        def st_d(s, ts):
            m = s % NM
            if ts[0] == 0:
                bank[s] = []
            for t in ts:
                ps = s1.tile([P, CH], BANK_DT, name="bank", tag="bank")
                nc.tensor.matmul_mx(
                    out=ps[:],
                    lhsT=w2c[:, m, P * t:P * (t + 1)].bitcast(FP8X4),
                    lhsT_scale=w2s[:, m, P * t:P * (t + 1)],
                    rhs=c1[s][:].bitcast(FP8X4),
                    rhs_scale=sc1[s][:],
                    start=True, stop=True,
                )
                bank[s].append(ps)

        def st_e(s):
            m = s % NM
            h2raw[s] = work.tile([P, 4, CH], BF16, name="h2raw", tag="h2raw", bufs=3)
            for t in range(4):
                nc.scalar.activation(
                    out=h2raw[s][:, t, :], in_=bank[s][t][:], func=ACT.Relu,
                    bias=b2c[:, m, t:t + 1], scale=1.0,
                )

        def st_f(s):
            g2[s] = work.tile([P, CH, 4], BF16, name="g2", tag="g2", bufs=2, align_bytes=64)
            nc.vector.tensor_copy(out=g2[s][:], in_=h2raw[s][:].rearrange("p t n -> p n t"))

        def st_g(s):
            c2[s] = work.tile([P, CH], U32, name="c2", tag="c2", bufs=7, align_bytes=64)
            sc2[s] = work.tile([P, CH], U8, name="sc2", tag="sc2", bufs=7, align_bytes=64)
            nc.vector.quantize_mx(
                out=c2[s][:].bitcast(FP8X4), scales=sc2[s][:],
                in_=g2[s][:].rearrange("p n t -> p (n t)"),
            )

        def plain_dummy(n):
            for i in range(n):
                junk = s1.tile([P, CH], F32, name="junk", tag="bank")
                nc.tensor.matmul(out=junk[:], lhsT=zl[:], rhs=zr[:], start=True, stop=True)

        def get_pbank(s):
            if s not in pbank:
                pbank[s] = s2.tile([P, 4, O2], F32, name="pbank", tag="pbank")
            return pbank[s]

        def mx_dummy(s):
            nc.tensor.matmul_mx(
                out=get_pbank(s)[:].rearrange("p j o -> p (j o)"),
                lhsT=c2[s - 1][:, 0:P].bitcast(FP8X4),
                lhsT_scale=sc2[s - 1][:, 0:P],
                rhs=w3c[:, 0:CH].bitcast(FP8X4),
                rhs_scale=w3s[:, 0:CH],
                start=True, stop=True,
            )

        def st_h(s):
            m = s % NM
            get_pbank(s)
            for j in range(4):
                nc.tensor.matmul_mx(
                    out=pbank[s][:, j, :],
                    lhsT=c2[s][:, P * j:P * (j + 1)].bitcast(FP8X4),
                    lhsT_scale=sc2[s][:, P * j:P * (j + 1)],
                    rhs=w3c[:, O2 * m:O2 * (m + 1)].bitcast(FP8X4),
                    rhs_scale=w3s[:, O2 * m:O2 * (m + 1)],
                    start=True, stop=True,
                )

        def st_hsum(c):
            psums[c] = aux.tile([P, 4, O2], F32, name="psum_all", tag="xw")
            for j in range(4):
                for m in range(NM):
                    s = c * NM + m
                    nc.tensor.matmul_mx(
                        out=psums[c][:, j, :],
                        lhsT=c2[s][:, P * j:P * (j + 1)].bitcast(FP8X4),
                        lhsT_scale=sc2[s][:, P * j:P * (j + 1)],
                        rhs=w3c[:, O2 * m:O2 * (m + 1)].bitcast(FP8X4),
                        rhs_scale=w3s[:, O2 * m:O2 * (m + 1)],
                        start=(m == 0), stop=(m == NM - 1),
                    )

        def bias_mean():
            nc.vector.tensor_reduce(
                out=bsum[:], in_=b3b[:, :, 0:O].rearrange("p m o -> p o m"),
                axis=mybir.AxisListType.X, op=ALU.add)
            nc.vector.tensor_scalar(
                out=bbar[:, 0, :], in0=bsum[:], scalar1=0.2, scalar2=None, op0=ALU.mult)

        def st_i(s):
            m = s % NM
            ys[s] = work.tile([P, 4, O2], F32, name="ys", tag="ys", bufs=4)
            nc.vector.tensor_tensor(
                out=ys[s][:], in0=pbank[s][:],
                in1=b3b[:, m:m + 1, :].to_broadcast([P, 4, O2]), op=ALU.add,
            )

        def st_js(s):
            sqs[s] = work.tile([P, 4, O], F32, name="sqs", tag="sqs", bufs=2)
            ab = work.tile([P, 4, O], F32, name="ab", tag="ab", bufs=2)
            exs[s] = work.tile([P, 4, O], F32, name="exs", tag="exs", bufs=2)
            nc.scalar.activation(out=ab[:], in_=ys[s][:, :, O:O2], func=ACT.Abs)
            nc.scalar.activation(out=sqs[s][:], in_=ys[s][:, :, 0:O], func=ACT.Square)
            nc.scalar.activation(out=exs[s][:], in_=ab[:], func=ACT.Exp, scale=-1.0)

        def st_mean(c):
            means[c] = work.tile([P, 4, O], F32, name="mean_sb", tag="mean_sb", bufs=2)
            msqs[c] = work.tile([P, 4, O], F32, name="msq", tag="msq", bufs=2)
            nc.vector.scalar_tensor_tensor(
                out=means[c][:], in0=psums[c][:, :, 0:O], scalar=0.2,
                in1=bbar[:].to_broadcast([P, 4, O]), op0=ALU.mult, op1=ALU.add)
            nc.sync.dma_start(
                out=out_0[c * CH:(c + 1) * CH, :].rearrange("(p j) o -> p j o", j=4),
                in_=means[c][:])

        def st_msq(c):
            nc.vector.tensor_tensor(out=msqs[c][:], in0=means[c][:], in1=means[c][:], op=ALU.mult)

        def st_u(c):
            nc.vector.scalar_tensor_tensor(
                out=upre[:, c], in0=accs[c][:], scalar=0.2, in1=msqs[c][:],
                op0=ALU.mult, op1=ALU.subtract)

        def st_jv(s):
            c, m = s // NM, s % NM
            v = ys[s][:, :, O:O2]
            if m == 0:
                accs[c] = work.tile([P, 4, O], F32, name="accs", tag="accs", bufs=2)
                nc.vector.tensor_scalar(
                    out=accp[:, c], in0=exs[s][:], scalar1=1.0, scalar2=None, op0=ALU.add)
                nc.vector.scalar_tensor_tensor(
                    out=accs[c][:], in0=v, scalar=0.0, in1=sqs[s][:], op0=ALU.max, op1=ALU.add)
                return
            nc.vector.scalar_tensor_tensor(
                out=accs[c][:], in0=v, scalar=0.0, in1=accs[c][:], op0=ALU.max, op1=ALU.add)
            nc.vector.scalar_tensor_tensor(
                out=accp[:, c], in0=exs[s][:], scalar=1.0, in1=accp[:, c], op0=ALU.add, op1=ALU.mult)
            nc.vector.tensor_tensor(out=accs[c][:], in0=sqs[s][:], in1=accs[c][:], op=ALU.add)

        def flat(t, c0, c1_):
            return t[:, c0:c1_].rearrange("p c j o -> p (c j o)")

        def fin_ln(c0, c1_):
            nc.scalar.activation(out=flat(lnp, c0, c1_), in_=flat(accp, c0, c1_), func=ACT.Ln)

        def fin_w(c0, c1_):
            nc.vector.scalar_tensor_tensor(
                out=flat(wv, c0, c1_), in0=flat(lnp, c0, c1_), scalar=0.2, in1=flat(upre, c0, c1_),
                op0=ALU.mult, op1=ALU.add)

        def fin_v(c0, c1_):
            nc.vector.tensor_scalar(
                out=flat(var_sb, c0, c1_), in0=flat(wv, c0, c1_), scalar1=-1e-6, scalar2=2e-6,
                op0=ALU.max, op1=ALU.add)
            nc.sync.dma_start(
                out=out_1.rearrange("(c p j) o -> p c (j o)", c=NCH, j=4)[:, c0:c1_, :],
                in_=var_sb[:, c0:c1_].rearrange("p c j o -> p c (j o)"))

        def w2_t(m, half):
            xt_w[(m, half)] = transposes(aux, "xw", words_of(raw_w2[m]), 512 * half, 2)
            if half == 1:
                freed()

        def w2_copy(m, half):
            if half == 0:
                wgs[m] = work.tile([P, H, 4], BF16, name="wg", tag="wg", bufs=2, align_bytes=64)
            copy_out(half == 0, wgs[m], 256 * half, xt_w[(m, half)], 256)

        def w2_q(m):
            nc.vector.quantize_mx(
                out=w2c[:, m, :].bitcast(FP8X4), scales=w2s[:, m, :],
                in_=wgs[m][:].rearrange("p n t -> p (n t)"),
            )

        def w3_prep(q):
            count = min(2, NM - 2 * q)
            ncols = P * count
            w = w3raw[:].rearrange("p m k -> p (m k)").bitcast(F32)
            xt = transposes(aux, "xw", w, 512 * q, count)
            copy_out(False, w3g, 256 * q, xt, ncols)
            nc.vector.quantize_mx(
                out=w3c[:, 256 * q:256 * q + ncols].bitcast(FP8X4),
                scales=w3s[:, 256 * q:256 * q + ncols],
                in_=w3g[:].rearrange("p n t -> p (n t)")[:, 1024 * q:1024 * q + 4 * ncols],
            )

        def ok(s):
            return 0 <= s < NS

        pump()
        plain_dummy(6)
        w2_t(0, 0)
        w2_copy(0, 0)
        plain_dummy(2)
        w2_t(0, 1)
        w2_copy(0, 1)
        w2_q(0)
        plain_dummy(2)
        st_a(0, 0)
        st_a(0, 1)
        plain_dummy(2)
        for k in range(-1, NS + 3):
            wm = k + 1
            has_w = 1 <= wm < NM
            junk_ok = 2 <= k <= NS
            chunk_mean = ok(k - 2) and (k - 2) % NM == NM - 1
            if ok(k + 1):
                st_b(k + 1)
            if k == 0:
                nc.scalar.dma_start(
                    out=b3b[:].rearrange("p m o -> p (m o)"),
                    in_=b3.rearrange("m o -> (m o)").partition_broadcast(P),
                )
            if ok(k - 2) and k < NS:
                st_i(k - 2)
            if ok(k - 4) and (k - 4) % NM == NM - 1:
                st_u((k - 4) // NM)
            if k == 3:
                bias_mean()
            if chunk_mean and k < NS:
                st_mean((k - 2) // NM)
            if ok(k - 1):
                st_f(k - 1)
            if ok(k - 2) and k >= NS:
                st_i(k - 2)
            if chunk_mean and k >= NS:
                st_mean((k - 2) // NM)
            if ok(k + 1):
                st_c(k + 1)
            if chunk_mean and k < NS:
                st_msq((k - 2) // NM)
            if ok(k):
                st_d(k, [0, 1])
            if has_w:
                w2_t(wm, 0)
                w2_copy(wm, 0)
            if ok(k + 2):
                st_a(k + 2, 0)
            if ok(k):
                st_d(k, [2])
            if junk_ok:
                mx_dummy(k - 1)
            if has_w:
                w2_t(wm, 1)
                w2_copy(wm, 1)
            if ok(k - 1):
                st_g(k - 1)
            if has_w:
                w2_q(wm)
            if ok(k + 2):
                st_a(k + 2, 1)
            if ok(k):
                st_d(k, [3])
            if 0 <= k < 3:
                w3_prep(k)
            if junk_ok:
                mx_dummy(k - 1)
            if ok(k - 1):
                st_h(k - 1)
                if (k - 1) % NM == NM - 1:
                    st_hsum((k - 1) // NM)
            if k < 0:
                plain_dummy(2)
            if ok(k - 3):
                st_js(k - 3)
            if ok(k):
                st_e(k)
            if ok(k - 3):
                st_jv(k - 3)
            if chunk_mean and k >= NS:
                st_msq((k - 2) // NM)
        st_u(NCH - 1)
        fin_ln(0, NCH - 1)
        fin_ln(NCH - 1, NCH)
        fin_w(0, NCH - 1)
        fin_w(NCH - 1, NCH)
        fin_v(0, NCH - 1)
        fin_v(NCH - 1, NCH)
